import numpy as np
import ml_dtypes


def mxq(x, axis, fmt="e4m3"):
    dtype, down = {"e4m3": (ml_dtypes.float8_e4m3fn, 7), "e5m2": (ml_dtypes.float8_e5m2, 14)}[fmt]
    v = np.moveaxis(np.asarray(x, np.float32).astype(ml_dtypes.bfloat16).astype(np.float64), axis, -1)
    blocks = v.reshape(v.shape[:-1] + (-1, 32))
    amax = np.abs(blocks).max(-1, keepdims=True)
    byte = np.maximum(np.where(amax > 0, np.frexp(amax)[1] - 1 + 127, 0) - down, 1)
    scale = np.exp2(byte - 127.0)
    codes = (blocks / scale).astype(np.float32).astype(dtype).astype(np.float64)
    return np.moveaxis((codes * scale).reshape(v.shape), -1, axis)


WIDE = False


def mx_kscale(k):
    if not WIDE:
        return np.ones(k)
    levels = np.array([10, -10, 5, -5, 0])
    if k % 512:
        return np.exp2(np.random.permutation(np.resize(levels, k // 32))).repeat(32)
    a = np.empty((k // 512, 16))
    for p in range(k // 512):
        a[p, :8] = np.random.permutation(np.resize(levels, 8))
        for g in range(8):
            far = levels[np.abs(levels - a[p, g]) >= 10]
            a[p, g + 8] = far[np.random.randint(len(far))]
    return np.exp2(a.ravel()).repeat(32)


BF16 = ml_dtypes.bfloat16


def bf(x):
    return np.asarray(x, np.float32).astype(BF16)


def f64(x):
    return np.asarray(x).astype(np.float64)


B, S, D, H, DH, F = 2, 128, 2048, 16, 128, 4096
E = H * DH
EPS = 1e-5


def layernorm(x, g, b):
    mu = x.mean(-1, keepdims=True)
    var = np.square(x - mu).mean(-1, keepdims=True)
    return (x - mu) / np.sqrt(var + EPS) * g + b


def make_pe():
    position = np.arange(S)[:, None] * 1.0
    div_term = np.exp(np.arange(0, DH, 2) * -(np.log(10000.0) / DH))
    pe = np.zeros((S, DH))
    pe[:, 0::2] = np.sin(position * div_term)
    pe[:, 1::2] = np.cos(position * div_term)
    return pe


def rope(t, pe):
    tr = t.reshape(B, H, S, DH // 2, 2)
    c = pe[:S, 0::2][None, None]
    d = pe[:S, 1::2][None, None]
    t0 = tr[..., 0] * c - tr[..., 1] * d
    t1 = tr[..., 0] * d + tr[..., 1] * c
    return np.stack([t0, t1], axis=-1).reshape(B, H, S, DH)


def setup_inputs():
    s = mx_kscale(D)
    x = np.random.standard_normal((B, S, D)) + 0.5 * np.random.standard_normal((B, S, 1))
    return {"x": bf(x),
            "pe": bf(make_pe()),
            "w_qkv": bf(np.random.standard_normal((3 * E, D)) / np.sqrt(D) / s),
            "g1": bf((1.0 + 0.1 * np.random.standard_normal(D)) * s),
            "b1": bf(0.1 * np.random.standard_normal(D) * s)}


def reference(x, pe, w_qkv, g1, b1):
    h = layernorm(f64(x), f64(g1), f64(b1))
    qkv = mxq(h, 2, "e4m3") @ mxq(f64(w_qkv), 1, "e4m3").T
    qkv = qkv.reshape(B, S, 3, H, DH)
    q, k, v = [qkv[:, :, i].transpose(0, 2, 1, 3) for i in range(3)]
    p = f64(pe)
    return rope(q, p), rope(k, p), v

@@ -1,0 +1,286 @@
+from contextlib import ExitStack
+
+import concourse.mybir as mybir
+from concourse.masks import make_identity
+
+F32 = mybir.dt.float32
+BF16 = mybir.dt.bfloat16
+I32 = mybir.dt.int32
+U32 = mybir.dt.uint32
+U8 = mybir.dt.uint8
+FP8X4 = mybir.dt.float8_e4m3fn_x4
+ALU = mybir.AluOpType
+
+P = 128
+BATCH = 2
+D = 2048
+HEADS = 16
+E = HEADS * P
+EPS = 1e-5
+PACK = 4
+PASSES = D // (P * PACK)
+BANK = 512
+GROUP = BANK
+ROWS = GROUP // P
+GROUP_HEADS = GROUP // P
+WORDS = D // 2
+PREFETCH = 4
+AHEAD = 2
+HALF = PASSES // 2
+LAG = 2
+
+FLOPS = 2 * BATCH * P * D * 3 * E
+
+
+def tile_minitransformerlayer_pa_kernel(tc, x, pe, w_qkv, g1, b1, out_0, out_1, out_2):
+    nc = tc.nc
+    outs = (out_0, out_1, out_2)
+    groups = [(part, head_group) for head_group in range(HEADS // GROUP_HEADS) for part in range(3)]
+
+    with ExitStack() as ctx:
+        const = ctx.enter_context(tc.tile_pool(name="const", bufs=1))
+        norm = ctx.enter_context(tc.tile_pool(name="norm", bufs=BATCH))
+        raw_pool = ctx.enter_context(tc.tile_pool(name="raw", bufs=PREFETCH))
+        grouped_pool = ctx.enter_context(tc.tile_pool(name="grouped", bufs=4))
+        codes_pool = ctx.enter_context(tc.tile_pool(name="codes", bufs=6))
+        rot_pool = ctx.enter_context(tc.tile_pool(name="rot", bufs=3))
+        result_pool = ctx.enter_context(tc.tile_pool(name="result", bufs=8))
+        flip_psum = ctx.enter_context(tc.psum_pool(name="flip_psum", bufs=6))
+        acc_psum = ctx.enter_context(tc.psum_pool(name="acc_psum", bufs=2))
+        ctx.enter_context(tc.manual_schedule())
+
+        one = const.tile([P, 1], F32)
+        nc.vector.memset(one[:], 1.0)
+        warm = const.tile([P, 1], F32)
+        nc.scalar.sqrt(out=warm[:], in_=one[:])
+        ones = const.tile([P, P], BF16)
+        nc.vector.memset(ones[:], 1.0)
+        gain_row = const.tile([P, D], BF16)
+        bias_row = const.tile([P, D], BF16)
+        nc.vector.memset(gain_row[:].bitcast(I32), 0)
+        nc.vector.memset(bias_row[:].bitcast(I32), 0)
+        pe_sb = const.tile([P, P], BF16)
+        ident_f32 = const.tile([P, P], F32)
+        make_identity(nc, ident_f32[:])
+        ident_bf16 = const.tile([P, P], BF16)
+        make_identity(nc, ident_bf16[:])
+
+        x_sb = {}
+        for b in range(BATCH):
+            x_tile = norm.tile([P, D], BF16, name="x_tile")
+            for c in range(D // BANK):
+                cols = slice(c * BANK, (c + 1) * BANK)
+                nc.sync.dma_start(out=x_tile[:, cols], in_=x[b][:, cols])
+            x_sb[b] = x_tile
+        nc.sync.dma_start(out=gain_row[0:1, :], in_=g1.rearrange("(o d) -> o d", o=1))
+        nc.sync.dma_start(out=bias_row[0:1, :], in_=b1.rearrange("(o d) -> o d", o=1))
+        nc.sync.dma_start(out=pe_sb[:], in_=pe)
+
+        w_raw = {}
+
+        def load_weights(n):
+            part, head_group = groups[n]
+            first = part * E + head_group * GROUP
+            raw = raw_pool.tile([P, ROWS * D], BF16, name="raw")
+            nc.sync.dma_start(
+                out=raw[:], in_=w_qkv[first : first + GROUP, :].rearrange("(p r) k -> p (r k)", r=ROWS)
+            )
+            w_raw[n] = raw
+
+        for n in range(PREFETCH):
+            load_weights(n)
+
+        pe_heads = pe_sb[:].unsqueeze(1).to_broadcast([P, GROUP_HEADS, P])
+        pe_pairs = (
+            pe_sb[:].rearrange("p (j i) -> p j i", i=2).unsqueeze(1).to_broadcast([P, GROUP_HEADS, P // 2, 2])
+        )
+        table_a = const.tile([P, GROUP_HEADS, P], F32)
+        nc.gpsimd.tensor_copy(out=table_a[:], in_=pe_heads)
+        table_b = const.tile([P, GROUP_HEADS, P // 2, 2], F32)
+        nc.gpsimd.tensor_scalar(
+            out=table_b[:, :, :, 0], in0=pe_pairs[:, :, :, 1], scalar1=-1.0, scalar2=0.0, op0=ALU.mult, op1=ALU.add
+        )
+        nc.gpsimd.tensor_copy(out=table_b[:, :, :, 1], in_=pe_pairs[:, :, :, 0])
+
+        def repeat_on_partitions(row, name):
+            repeated = const.tile([P, D], BF16, name=name)
+            for bank in range(D // (2 * BANK)):
+                spread = flip_psum.tile([P, 2 * BANK], BF16, tag="flipped", name="spread")
+                for side in range(2):
+                    first = (2 * bank + side) * BANK
+                    nc.tensor.matmul(
+                        out=spread[:, side * BANK : (side + 1) * BANK],
+                        lhsT=ones[:],
+                        rhs=row[:, first : first + BANK],
+                        start=True,
+                        stop=True,
+                    )
+                nc.scalar.copy(out=repeated[:, 2 * bank * BANK : 2 * (bank + 1) * BANK], in_=spread[:])
+            return repeated
+
+        gain = repeat_on_partitions(gain_row, "gain")
+        bias = repeat_on_partitions(bias_row, "bias")
+
+        mean_var = {}
+        std = {}
+
+        def token_statistics(b):
+            stats = norm.tile([P, D // BANK, 6], F32, name="stats")
+            for c in range(D // BANK):
+                nc.vector.bn_stats(out=stats[:, c, :], in_=x_sb[b][:, c * BANK : (c + 1) * BANK])
+            mv = norm.tile([P, 2], F32, name="mv")
+            nc.vector.bn_aggr(out=mv[:], in_=stats[:].rearrange("p c s -> p (c s)"))
+            var_eps = norm.tile([P, 1], F32, name="var_eps")
+            nc.vector.tensor_scalar_add(out=var_eps[:], in0=mv[:, 1:2], scalar1=EPS)
+            root = norm.tile([P, 1], F32, name="root")
+            nc.scalar.sqrt(out=root[:], in_=var_eps[:])
+            mean_var[b] = mv
+            std[b] = root
+
+        h_sorted = {}
+
+        def normalise(b):
+            centred = const.tile([P, D], F32, name="centred")
+            nc.vector.scalar_tensor_tensor(
+                out=centred[:], in0=x_sb[b][:], scalar=mean_var[b][:, 0:1], in1=gain[:], op0=ALU.subtract, op1=ALU.mult
+            )
+            rstd = norm.tile([P, 1], F32, name="rstd")
+            nc.vector.reciprocal(out=rstd[:], in_=std[b][:])
+            h_tile = norm.tile([P, PASSES, PACK, P], BF16, name="h_tile")
+            for t in range(PACK):
+                nc.vector.scalar_tensor_tensor(
+                    out=h_tile[:, :, t, :],
+                    in0=centred[:].rearrange("p (c q t) -> p c t q", q=P, t=PACK)[:, :, t, :],
+                    scalar=rstd[:],
+                    in1=bias[:].rearrange("p (c q t) -> p c t q", q=P, t=PACK)[:, :, t, :],
+                    op0=ALU.mult,
+                    op1=ALU.add,
+                )
+            h_sorted[b] = h_tile
+
+        h_grouped = const.tile([P, BATCH, PASSES, P, PACK], BF16, align_bytes=64)
+        h_codes = const.tile([P, BATCH, PASSES * P], U32, align_bytes=64)
+        h_scales = const.tile([P, BATCH, PASSES * P], U8, align_bytes=64)
+
+        def transpose_h(b):
+            for c in range(PASSES):
+                flipped_h = flip_psum.tile([P, PACK, P], BF16, tag="flipped", name="flipped_h")
+                for t in range(PACK):
+                    nc.tensor.transpose(flipped_h[:, t, :], h_sorted[b][:, c, t, :], ident_bf16[:])
+                nc.scalar.copy(out=h_grouped[:, b, c, :, :], in_=flipped_h[:].rearrange("p t r -> p r t"))
+
+        def quantise_h(b):
+            nc.vector.quantize_mx(
+                out=h_codes[:, b, :].bitcast(FP8X4),
+                scales=h_scales[:, b, :],
+                in_=h_grouped[:, b].rearrange("p c r t -> p (c r t)"),
+            )
+
+        w_grouped = {}
+
+        def transpose_weights(n, half):
+            words = w_raw[n][:].bitcast(F32)
+            grouped = grouped_pool.tile([P, HALF, GROUP * PACK], BF16, align_bytes=64, name="grouped")
+            for c in range(HALF):
+                grouped_words = grouped[:, c, :].bitcast(F32)
+                for side in range(2):
+                    flipped = flip_psum.tile([P, 2, BANK // 2], F32, tag="flipped", name="flipped")
+                    for u in range(2):
+                        for r in range(2):
+                            first = (2 * side + r) * WORDS + 2 * (half * HALF + c) * P
+                            nc.tensor.transpose(
+                                flipped[:, u, r * P : (r + 1) * P], words[:, first + u : first + 2 * P : 2], ident_f32[:]
+                            )
+                    nc.scalar.copy(
+                        out=grouped_words[:, side * BANK : (side + 1) * BANK].rearrange("p (n u) -> p n u", u=2),
+                        in_=flipped[:].rearrange("p u n -> p n u"),
+                    )
+            w_grouped[(n, half)] = grouped
+            if half == 1 and n + PREFETCH < len(groups):
+                load_weights(n + PREFETCH)
+
+        w_codes = {}
+        w_scales = {}
+
+        def quantise_weights(n, half):
+            codes = codes_pool.tile([P, HALF, GROUP], U32, align_bytes=64, name="codes")
+            scales = codes_pool.tile([P, HALF, GROUP], U8, align_bytes=64, name="scales")
+            nc.vector.quantize_mx(
+                out=codes[:].rearrange("p c n -> p (c n)").bitcast(FP8X4),
+                scales=scales[:].rearrange("p c n -> p (c n)"),
+                in_=w_grouped[(n, half)][:].rearrange("p c n -> p (c n)"),
+            )
+            w_codes[(n, half)] = codes
+            w_scales[(n, half)] = scales
+
+        products = {}
+
+        def multiply(n, b):
+            acc = acc_psum.tile([P, BANK], F32, name="acc")
+            for c in range(PASSES):
+                tokens = slice(c * P, (c + 1) * P)
+                nc.tensor.matmul_mx(
+                    out=acc[:],
+                    lhsT=h_codes[:, b, tokens].bitcast(FP8X4),
+                    lhsT_scale=h_scales[:, b, tokens],
+                    rhs=w_codes[(n, c // HALF)][:, c % HALF, :].bitcast(FP8X4),
+                    rhs_scale=w_scales[(n, c // HALF)][:, c % HALF, :],
+                    start=(c == 0),
+                    stop=(c == PASSES - 1),
+                )
+            products[(n, b)] = acc
+
+        def finish(n, b):
+            part, head_group = groups[n]
+            heads = slice(head_group * GROUP_HEADS, (head_group + 1) * GROUP_HEADS)
+            acc = products[(n, b)]
+            result = result_pool.tile([P, GROUP], F32, name="result")
+            if part == 2:
+                nc.vector.tensor_copy(
+                    out=result[:].rearrange("s (p r) -> s p r", r=ROWS),
+                    in_=acc[:].rearrange("s (r p) -> s p r", r=ROWS),
+                )
+            else:
+                pairs = acc[:].rearrange("s (v i p) -> s i p v", v=2, i=2)
+                shape = [P, P, 2, 2]
+                from_a = rot_pool.tile([P, GROUP], F32, name="from_a")
+                nc.vector.tensor_mul(
+                    out=from_a[:].rearrange("s (p v i) -> s p v i", v=2, i=2),
+                    in0=pairs[:, 0].unsqueeze(3).to_broadcast(shape),
+                    in1=table_a[:].rearrange("s h (q v i) -> s (h q) v i", v=2, i=2),
+                )
+                from_b = rot_pool.tile([P, GROUP], F32, name="from_b")
+                nc.vector.tensor_mul(
+                    out=from_b[:].rearrange("s (p v i) -> s p v i", v=2, i=2),
+                    in0=pairs[:, 1].unsqueeze(3).to_broadcast(shape),
+                    in1=table_b[:].rearrange("s h (q v) i -> s (h q) v i", v=2),
+                )
+                nc.gpsimd.tensor_add(out=result[:], in0=from_a[:], in1=from_b[:])
+            nc.sync.dma_start(
+                out=outs[part][b, heads].rearrange("h s d -> s h d"),
+                in_=result[:].rearrange("s (h d) -> s h d", d=P),
+            )
+
+        halves = [(n, half) for n in range(len(groups)) for half in range(2)]
+        token_statistics(0)
+        token_statistics(1)
+        transpose_weights(0, 0)
+        transpose_weights(0, 1)
+        normalise(0)
+        transpose_h(0)
+        transpose_weights(1, 0)
+        transpose_weights(1, 1)
+        normalise(1)
+        transpose_h(1)
+        quantise_weights(0, 0)
+        quantise_weights(0, 1)
+        quantise_h(0)
+        quantise_h(1)
+        for t in range(len(halves)):
+            n, b = halves[t]
+            multiply(n, b)
+            if t + 2 * AHEAD - LAG < len(halves):
+                quantise_weights(*halves[t + 2 * AHEAD - LAG])
+            finish(n, b)
+            if t + 2 * AHEAD < len(halves):
+                transpose_weights(*halves[t + 2 * AHEAD])

@@ -25,9 +25,8 @@ ROWS = GROUP // P
 GROUP_HEADS = GROUP // P
 WORDS = D // 2
 PREFETCH = 4
-AHEAD = 2
+LEAD = 5
 HALF = PASSES // 2
-LAG = 2
 
 FLOPS = 2 * BATCH * P * D * 3 * E
 
@@ -41,53 +40,65 @@ def tile_minitransformerlayer_pa_kernel(tc, x, pe, w_qkv, g1, b1, out_0, out_1, 
         const = ctx.enter_context(tc.tile_pool(name="const", bufs=1))
         norm = ctx.enter_context(tc.tile_pool(name="norm", bufs=BATCH))
         raw_pool = ctx.enter_context(tc.tile_pool(name="raw", bufs=PREFETCH))
-        grouped_pool = ctx.enter_context(tc.tile_pool(name="grouped", bufs=4))
-        codes_pool = ctx.enter_context(tc.tile_pool(name="codes", bufs=6))
+        grouped_pool = ctx.enter_context(tc.tile_pool(name="grouped", bufs=5))
+        codes_pool = ctx.enter_context(tc.tile_pool(name="codes", bufs=8))
         rot_pool = ctx.enter_context(tc.tile_pool(name="rot", bufs=3))
-        result_pool = ctx.enter_context(tc.tile_pool(name="result", bufs=8))
+        result_pool = ctx.enter_context(tc.tile_pool(name="result", bufs=6))
         flip_psum = ctx.enter_context(tc.psum_pool(name="flip_psum", bufs=6))
         acc_psum = ctx.enter_context(tc.psum_pool(name="acc_psum", bufs=2))
         ctx.enter_context(tc.manual_schedule())
 
+        gain_row = const.tile([P, D], BF16)
+        bias_row = const.tile([P, D], BF16)
+        nc.vector.memset(gain_row[:].bitcast(I32), 0)
+        ones = const.tile([P, P], BF16)
+        nc.vector.memset(ones[:], 1.0)
+        nc.vector.memset(bias_row[:].bitcast(I32), 0)
         one = const.tile([P, 1], F32)
         nc.vector.memset(one[:], 1.0)
         warm = const.tile([P, 1], F32)
         nc.scalar.sqrt(out=warm[:], in_=one[:])
-        ones = const.tile([P, P], BF16)
-        nc.vector.memset(ones[:], 1.0)
-        gain_row = const.tile([P, D], BF16)
-        bias_row = const.tile([P, D], BF16)
-        nc.vector.memset(gain_row[:].bitcast(I32), 0)
-        nc.vector.memset(bias_row[:].bitcast(I32), 0)
         pe_sb = const.tile([P, P], BF16)
         ident_f32 = const.tile([P, P], F32)
         make_identity(nc, ident_f32[:])
-        ident_bf16 = const.tile([P, P], BF16)
-        make_identity(nc, ident_bf16[:])
 
         x_sb = {}
+
+        def load_tokens(b, c):
+            cols = slice(c * BANK, (c + 1) * BANK)
+            nc.sync.dma_start(out=x_sb[b][:, cols], in_=x[b][:, cols])
+
         for b in range(BATCH):
             x_tile = norm.tile([P, D], BF16, name="x_tile")
-            for c in range(D // BANK):
-                cols = slice(c * BANK, (c + 1) * BANK)
-                nc.sync.dma_start(out=x_tile[:, cols], in_=x[b][:, cols])
             x_sb[b] = x_tile
-        nc.sync.dma_start(out=gain_row[0:1, :], in_=g1.rearrange("(o d) -> o d", o=1))
-        nc.sync.dma_start(out=bias_row[0:1, :], in_=b1.rearrange("(o d) -> o d", o=1))
-        nc.sync.dma_start(out=pe_sb[:], in_=pe)
 
         w_raw = {}
 
-        def load_weights(n):
+        def load_weights(n, pieces=1):
             part, head_group = groups[n]
             first = part * E + head_group * GROUP
             raw = raw_pool.tile([P, ROWS * D], BF16, name="raw")
-            nc.sync.dma_start(
-                out=raw[:], in_=w_qkv[first : first + GROUP, :].rearrange("(p r) k -> p (r k)", r=ROWS)
-            )
+            rows = w_qkv[first : first + GROUP, :].rearrange("(p r) k -> p r k", r=ROWS)
+            width = D // pieces
+            for piece in range(pieces):
+                cols = slice(piece * width, (piece + 1) * width)
+                nc.sync.dma_start(
+                    out=raw[:].rearrange("p (r k) -> p r k", r=ROWS)[:, :, cols], in_=rows[:, :, cols]
+                )
             w_raw[n] = raw
 
-        for n in range(PREFETCH):
+        load_tokens(0, 0)
+        load_tokens(0, 1)
+        nc.sync.dma_start(out=gain_row[0:1, :], in_=g1.rearrange("(o d) -> o d", o=1))
+        nc.sync.dma_start(out=bias_row[0:1, :], in_=b1.rearrange("(o d) -> o d", o=1))
+        load_tokens(0, 2)
+        load_tokens(0, 3)
+        load_weights(0, 2)
+        for c in range(D // BANK):
+            load_tokens(1, c)
+        nc.sync.dma_start(out=pe_sb[:], in_=pe)
+        load_weights(1, 2)
+        for n in range(2, PREFETCH):
             load_weights(n)
 
         pe_heads = pe_sb[:].unsqueeze(1).to_broadcast([P, GROUP_HEADS, P])
@@ -137,7 +148,7 @@ def tile_minitransformerlayer_pa_kernel(tc, x, pe, w_qkv, g1, b1, out_0, out_1, 
             mean_var[b] = mv
             std[b] = root
 
-        h_sorted = {}
+        h_rows = {}
 
         def normalise(b):
             centred = const.tile([P, D], F32, name="centred")
@@ -146,28 +157,33 @@ def tile_minitransformerlayer_pa_kernel(tc, x, pe, w_qkv, g1, b1, out_0, out_1, 
             )
             rstd = norm.tile([P, 1], F32, name="rstd")
             nc.vector.reciprocal(out=rstd[:], in_=std[b][:])
-            h_tile = norm.tile([P, PASSES, PACK, P], BF16, name="h_tile")
-            for t in range(PACK):
-                nc.vector.scalar_tensor_tensor(
-                    out=h_tile[:, :, t, :],
-                    in0=centred[:].rearrange("p (c q t) -> p c t q", q=P, t=PACK)[:, :, t, :],
-                    scalar=rstd[:],
-                    in1=bias[:].rearrange("p (c q t) -> p c t q", q=P, t=PACK)[:, :, t, :],
-                    op0=ALU.mult,
-                    op1=ALU.add,
-                )
-            h_sorted[b] = h_tile
+            h_tile = norm.tile([P, D], BF16, name="h_tile")
+            nc.vector.scalar_tensor_tensor(
+                out=h_tile[:], in0=centred[:], scalar=rstd[:], in1=bias[:], op0=ALU.mult, op1=ALU.add
+            )
+            h_rows[b] = h_tile
 
         h_grouped = const.tile([P, BATCH, PASSES, P, PACK], BF16, align_bytes=64)
         h_codes = const.tile([P, BATCH, PASSES * P], U32, align_bytes=64)
         h_scales = const.tile([P, BATCH, PASSES * P], U8, align_bytes=64)
 
         def transpose_h(b):
-            for c in range(PASSES):
-                flipped_h = flip_psum.tile([P, PACK, P], BF16, tag="flipped", name="flipped_h")
-                for t in range(PACK):
-                    nc.tensor.transpose(flipped_h[:, t, :], h_sorted[b][:, c, t, :], ident_bf16[:])
-                nc.scalar.copy(out=h_grouped[:, b, c, :, :], in_=flipped_h[:].rearrange("p t r -> p r t"))
+            words = h_rows[b][:].bitcast(F32)
+            for pair in range(HALF):
+                flipped_h = flip_psum.tile([P, HALF, 2, P], F32, tag="flipped", name="flipped_h")
+                for c in range(HALF):
+                    first = (pair * HALF + c) * 2 * P
+                    for u in range(2):
+                        nc.tensor.transpose(
+                            flipped_h[:, c, u, :], words[:, first + u : first + 2 * P : 2], ident_f32[:]
+                        )
+                nc.scalar.copy(
+                    out=h_grouped[:, b, pair * HALF : (pair + 1) * HALF, :, :]
+                    .rearrange("p c r t -> p (c r t)")
+                    .bitcast(F32)
+                    .rearrange("p (c r u) -> p c r u", c=HALF, u=2),
+                    in_=flipped_h[:].rearrange("p c u r -> p c r u"),
+                )
 
         def quantise_h(b):
             nc.vector.quantize_mx(
@@ -262,25 +278,35 @@ def tile_minitransformerlayer_pa_kernel(tc, x, pe, w_qkv, g1, b1, out_0, out_1, 
             )
 
         halves = [(n, half) for n in range(len(groups)) for half in range(2)]
+        products_order = [(0, 0)]
+        for n in range(1, len(groups)):
+            products_order += [(n, 0), (n - 1, 1)]
+        products_order.append((len(groups) - 1, 1))
         token_statistics(0)
-        token_statistics(1)
-        transpose_weights(0, 0)
-        transpose_weights(0, 1)
+        transpose_weights(*halves[0])
+        transpose_weights(*halves[1])
         normalise(0)
         transpose_h(0)
-        transpose_weights(1, 0)
-        transpose_weights(1, 1)
-        normalise(1)
-        transpose_h(1)
-        quantise_weights(0, 0)
-        quantise_weights(0, 1)
+        transpose_weights(*halves[2])
+        transpose_weights(*halves[3])
+        token_statistics(1)
+        quantise_weights(*halves[0])
+        quantise_weights(*halves[1])
         quantise_h(0)
+        multiply(*products_order[0])
+        transpose_weights(*halves[4])
+        normalise(1)
+        quantise_weights(*halves[2])
+        quantise_weights(*halves[3])
+        transpose_weights(*halves[5])
+        transpose_h(1)
         quantise_h(1)
-        for t in range(len(halves)):
-            n, b = halves[t]
-            multiply(n, b)
-            if t + 2 * AHEAD - LAG < len(halves):
-                quantise_weights(*halves[t + 2 * AHEAD - LAG])
-            finish(n, b)
-            if t + 2 * AHEAD < len(halves):
-                transpose_weights(*halves[t + 2 * AHEAD])
+        quantise_weights(*halves[4])
+        finish(*products_order[0])
+        for t in range(1, len(halves)):
+            multiply(*products_order[t])
+            if t + LEAD - 1 < len(halves):
+                quantise_weights(*halves[t + LEAD - 1])
+            finish(*products_order[t])
+            if t + LEAD < len(halves):
+                transpose_weights(*halves[t + LEAD])

@@ -194,10 +194,13 @@ def tile_minitransformerlayer_pa_kernel(tc, x, pe, w_qkv, g1, b1, out_0, out_1, 
 
         w_grouped = {}
 
-        def transpose_weights(n, half):
+        def transpose_weights(n, half, passes=range(HALF)):
             words = w_raw[n][:].bitcast(F32)
-            grouped = grouped_pool.tile([P, HALF, GROUP * PACK], BF16, align_bytes=64, name="grouped")
-            for c in range(HALF):
+            if 0 in passes:
+                grouped = grouped_pool.tile([P, HALF, GROUP * PACK], BF16, align_bytes=64, name="grouped")
+                w_grouped[(n, half)] = grouped
+            grouped = w_grouped[(n, half)]
+            for c in passes:
                 grouped_words = grouped[:, c, :].bitcast(F32)
                 for side in range(2):
                     flipped = flip_psum.tile([P, 2, BANK // 2], F32, tag="flipped", name="flipped")
@@ -211,8 +214,7 @@ def tile_minitransformerlayer_pa_kernel(tc, x, pe, w_qkv, g1, b1, out_0, out_1, 
                         out=grouped_words[:, side * BANK : (side + 1) * BANK].rearrange("p (n u) -> p n u", u=2),
                         in_=flipped[:].rearrange("p u n -> p n u"),
                     )
-            w_grouped[(n, half)] = grouped
-            if half == 1 and n + PREFETCH < len(groups):
+            if half == 1 and HALF - 1 in passes and n + PREFETCH < len(groups):
                 load_weights(n + PREFETCH)
 
         w_codes = {}
@@ -231,9 +233,12 @@ def tile_minitransformerlayer_pa_kernel(tc, x, pe, w_qkv, g1, b1, out_0, out_1, 
 
         products = {}
 
-        def multiply(n, b):
-            acc = acc_psum.tile([P, BANK], F32, name="acc")
-            for c in range(PASSES):
+        def multiply(n, b, passes=range(PASSES)):
+            if 0 in passes:
+                acc = acc_psum.tile([P, BANK], F32, name="acc")
+                products[(n, b)] = acc
+            acc = products[(n, b)]
+            for c in passes:
                 tokens = slice(c * P, (c + 1) * P)
                 nc.tensor.matmul_mx(
                     out=acc[:],
@@ -244,7 +249,6 @@ def tile_minitransformerlayer_pa_kernel(tc, x, pe, w_qkv, g1, b1, out_0, out_1, 
                     start=(c == 0),
                     stop=(c == PASSES - 1),
                 )
-            products[(n, b)] = acc
 
         def finish(n, b):
             part, head_group = groups[n]
@@ -304,9 +308,12 @@ def tile_minitransformerlayer_pa_kernel(tc, x, pe, w_qkv, g1, b1, out_0, out_1, 
         quantise_weights(*halves[4])
         finish(*products_order[0])
         for t in range(1, len(halves)):
-            multiply(*products_order[t])
+            for c in range(HALF):
+                multiply(*products_order[t], passes=range(c * HALF, (c + 1) * HALF))
+                if c == 0 and t + LEAD < len(halves):
+                    transpose_weights(*halves[t + LEAD], passes=(0,))
             if t + LEAD - 1 < len(halves):
                 quantise_weights(*halves[t + LEAD - 1])
             finish(*products_order[t])
             if t + LEAD < len(halves):
-                transpose_weights(*halves[t + LEAD])
+                transpose_weights(*halves[t + LEAD], passes=(1,))

@@ -40,10 +40,11 @@ def tile_minitransformerlayer_pa_kernel(tc, x, pe, w_qkv, g1, b1, out_0, out_1, 
         const = ctx.enter_context(tc.tile_pool(name="const", bufs=1))
         norm = ctx.enter_context(tc.tile_pool(name="norm", bufs=BATCH))
         raw_pool = ctx.enter_context(tc.tile_pool(name="raw", bufs=PREFETCH))
+        sorted_pool = ctx.enter_context(tc.tile_pool(name="sorted", bufs=3))
         grouped_pool = ctx.enter_context(tc.tile_pool(name="grouped", bufs=5))
         codes_pool = ctx.enter_context(tc.tile_pool(name="codes", bufs=8))
-        rot_pool = ctx.enter_context(tc.tile_pool(name="rot", bufs=3))
-        result_pool = ctx.enter_context(tc.tile_pool(name="result", bufs=6))
+        rot_pool = ctx.enter_context(tc.tile_pool(name="rot", bufs=2))
+        result_pool = ctx.enter_context(tc.tile_pool(name="result", bufs=4))
         flip_psum = ctx.enter_context(tc.psum_pool(name="flip_psum", bufs=6))
         acc_psum = ctx.enter_context(tc.psum_pool(name="acc_psum", bufs=2))
         ctx.enter_context(tc.manual_schedule())
@@ -193,6 +194,16 @@ def tile_minitransformerlayer_pa_kernel(tc, x, pe, w_qkv, g1, b1, out_0, out_1, 
             )
 
         w_grouped = {}
+        w_sorted = {}
+
+        def sort_words(n, half, c):
+            words = w_raw[n][:].bitcast(F32).rearrange("p (r w) -> p r w", r=ROWS)
+            first = 2 * (half * HALF + c) * P
+            in_order = sorted_pool.tile([P, ROWS, 2, P], F32, name="in_order")
+            nc.vector.tensor_copy(
+                out=in_order[:], in_=words[:, :, first : first + 2 * P].rearrange("p r (q u) -> p r u q", u=2)
+            )
+            w_sorted[(n, half, c)] = in_order
 
         def transpose_weights(n, half, passes=range(HALF)):
             words = w_raw[n][:].bitcast(F32)
@@ -207,9 +218,11 @@ def tile_minitransformerlayer_pa_kernel(tc, x, pe, w_qkv, g1, b1, out_0, out_1, 
                     for u in range(2):
                         for r in range(2):
                             first = (2 * side + r) * WORDS + 2 * (half * HALF + c) * P
-                            nc.tensor.transpose(
-                                flipped[:, u, r * P : (r + 1) * P], words[:, first + u : first + 2 * P : 2], ident_f32[:]
-                            )
+                            if (n, half, c) in w_sorted:
+                                column_words = w_sorted[(n, half, c)][:, 2 * side + r, u, :]
+                            else:
+                                column_words = words[:, first + u : first + 2 * P : 2]
+                            nc.tensor.transpose(flipped[:, u, r * P : (r + 1) * P], column_words, ident_f32[:])
                     nc.scalar.copy(
                         out=grouped_words[:, side * BANK : (side + 1) * BANK].rearrange("p (n u) -> p n u", u=2),
                         in_=flipped[:].rearrange("p u n -> p n u"),
@@ -256,7 +269,7 @@ def tile_minitransformerlayer_pa_kernel(tc, x, pe, w_qkv, g1, b1, out_0, out_1, 
             acc = products[(n, b)]
             result = result_pool.tile([P, GROUP], F32, name="result")
             if part == 2:
-                nc.vector.tensor_copy(
+                nc.scalar.copy(
                     out=result[:].rearrange("s (p r) -> s p r", r=ROWS),
                     in_=acc[:].rearrange("s (r p) -> s p r", r=ROWS),
                 )
@@ -307,6 +320,7 @@ def tile_minitransformerlayer_pa_kernel(tc, x, pe, w_qkv, g1, b1, out_0, out_1, 
         quantise_h(1)
         quantise_weights(*halves[4])
         finish(*products_order[0])
+        sort_words(*halves[1 + LEAD], 0)
         for t in range(1, len(halves)):
             for c in range(HALF):
                 multiply(*products_order[t], passes=range(c * HALF, (c + 1) * HALF))
@@ -315,5 +329,7 @@ def tile_minitransformerlayer_pa_kernel(tc, x, pe, w_qkv, g1, b1, out_0, out_1, 
             if t + LEAD - 1 < len(halves):
                 quantise_weights(*halves[t + LEAD - 1])
             finish(*products_order[t])
+            if t + LEAD + 1 < len(halves):
+                sort_words(*halves[t + LEAD + 1], 0)
             if t + LEAD < len(halves):
                 transpose_weights(*halves[t + LEAD], passes=(1,))

@@ -25,6 +25,7 @@ ROWS = GROUP // P
 GROUP_HEADS = GROUP // P
 WORDS = D // 2
 PREFETCH = 4
+SORT_FROM = 8
 LEAD = 5
 HALF = PASSES // 2
 
@@ -320,16 +321,15 @@ def tile_minitransformerlayer_pa_kernel(tc, x, pe, w_qkv, g1, b1, out_0, out_1, 
         quantise_h(1)
         quantise_weights(*halves[4])
         finish(*products_order[0])
-        sort_words(*halves[1 + LEAD], 0)
         for t in range(1, len(halves)):
             for c in range(HALF):
                 multiply(*products_order[t], passes=range(c * HALF, (c + 1) * HALF))
                 if c == 0 and t + LEAD < len(halves):
                     transpose_weights(*halves[t + LEAD], passes=(0,))
+            if SORT_FROM <= t + LEAD + 1 < len(halves):
+                sort_words(*halves[t + LEAD + 1], 0)
             if t + LEAD - 1 < len(halves):
                 quantise_weights(*halves[t + LEAD - 1])
             finish(*products_order[t])
-            if t + LEAD + 1 < len(halves):
-                sort_words(*halves[t + LEAD + 1], 0)
             if t + LEAD < len(halves):
                 transpose_weights(*halves[t + LEAD], passes=(1,))

@@ -44,7 +44,7 @@ def tile_minitransformerlayer_pa_kernel(tc, x, pe, w_qkv, g1, b1, out_0, out_1, 
         sorted_pool = ctx.enter_context(tc.tile_pool(name="sorted", bufs=3))
         grouped_pool = ctx.enter_context(tc.tile_pool(name="grouped", bufs=5))
         codes_pool = ctx.enter_context(tc.tile_pool(name="codes", bufs=8))
-        rot_pool = ctx.enter_context(tc.tile_pool(name="rot", bufs=2))
+        rot_pool = ctx.enter_context(tc.tile_pool(name="rot", bufs=3))
         result_pool = ctx.enter_context(tc.tile_pool(name="result", bufs=4))
         flip_psum = ctx.enter_context(tc.psum_pool(name="flip_psum", bufs=6))
         acc_psum = ctx.enter_context(tc.psum_pool(name="acc_psum", bufs=2))
@@ -249,7 +249,10 @@ def tile_minitransformerlayer_pa_kernel(tc, x, pe, w_qkv, g1, b1, out_0, out_1, 
 
         def multiply(n, b, passes=range(PASSES)):
             if 0 in passes:
-                acc = acc_psum.tile([P, BANK], F32, name="acc")
+                if n >= len(groups) - 1:
+                    acc = flip_psum.tile([P, BANK], F32, tag="flipped", name="acc")
+                else:
+                    acc = acc_psum.tile([P, BANK], F32, name="acc")
                 products[(n, b)] = acc
             acc = products[(n, b)]
             for c in passes:
@@ -264,9 +267,12 @@ def tile_minitransformerlayer_pa_kernel(tc, x, pe, w_qkv, g1, b1, out_0, out_1, 
                     stop=(c == PASSES - 1),
                 )
 
+        rotated = {}
+        waited = const.tile([P, 1], U32)
+        results = {}
+
         def finish(n, b):
-            part, head_group = groups[n]
-            heads = slice(head_group * GROUP_HEADS, (head_group + 1) * GROUP_HEADS)
+            part = groups[n][0]
             acc = products[(n, b)]
             result = result_pool.tile([P, GROUP], F32, name="result")
             if part == 2:
@@ -289,7 +295,16 @@ def tile_minitransformerlayer_pa_kernel(tc, x, pe, w_qkv, g1, b1, out_0, out_1, 
                     in0=pairs[:, 1].unsqueeze(3).to_broadcast(shape),
                     in1=table_b[:].rearrange("s h (q v) i -> s (h q) v i", v=2),
                 )
-                nc.gpsimd.tensor_add(out=result[:], in0=from_a[:], in1=from_b[:])
+                rotated[(n, b)] = (from_a, from_b)
+            results[(n, b)] = result
+
+        def add_and_store(n, b, engine):
+            part, head_group = groups[n]
+            heads = slice(head_group * GROUP_HEADS, (head_group + 1) * GROUP_HEADS)
+            result = results[(n, b)]
+            if part < 2:
+                from_a, from_b = rotated[(n, b)]
+                engine.tensor_add(out=result[:], in0=from_a[:], in1=from_b[:])
             nc.sync.dma_start(
                 out=outs[part][b, heads].rearrange("h s d -> s h d"),
                 in_=result[:].rearrange("s (h d) -> s h d", d=P),
@@ -321,6 +336,7 @@ def tile_minitransformerlayer_pa_kernel(tc, x, pe, w_qkv, g1, b1, out_0, out_1, 
         quantise_h(1)
         quantise_weights(*halves[4])
         finish(*products_order[0])
+        waiting = [products_order[0]]
         for t in range(1, len(halves)):
             for c in range(HALF):
                 multiply(*products_order[t], passes=range(c * HALF, (c + 1) * HALF))
@@ -330,6 +346,18 @@ def tile_minitransformerlayer_pa_kernel(tc, x, pe, w_qkv, g1, b1, out_0, out_1, 
                 sort_words(*halves[t + LEAD + 1], 0)
             if t + LEAD - 1 < len(halves):
                 quantise_weights(*halves[t + LEAD - 1])
+            if groups[products_order[t][0]][0] < 2:
+                if t + LEAD - 1 < len(halves):
+                    nc.gpsimd.tensor_copy(out=waited[:], in_=w_codes[halves[t + LEAD - 1]][:, 0, 0:1])
+                for product in waiting:
+                    add_and_store(*product, nc.gpsimd)
+                waiting = []
             finish(*products_order[t])
+            if groups[products_order[t][0]][0] < 2:
+                waiting.append(products_order[t])
+            else:
+                add_and_store(*products_order[t], nc.gpsimd)
             if t + LEAD < len(halves):
                 transpose_weights(*halves[t + LEAD], passes=(1,))
+        for product in waiting:
+            add_and_store(*product, nc.vector)

@@ -26,7 +26,7 @@ GROUP_HEADS = GROUP // P
 WORDS = D // 2
 PREFETCH = 4
 SORT_FROM = 8
-LEAD = 5
+LEAD = 6
 HALF = PASSES // 2
 
 FLOPS = 2 * BATCH * P * D * 3 * E
@@ -41,8 +41,8 @@ def tile_minitransformerlayer_pa_kernel(tc, x, pe, w_qkv, g1, b1, out_0, out_1, 
         const = ctx.enter_context(tc.tile_pool(name="const", bufs=1))
         norm = ctx.enter_context(tc.tile_pool(name="norm", bufs=BATCH))
         raw_pool = ctx.enter_context(tc.tile_pool(name="raw", bufs=PREFETCH))
-        sorted_pool = ctx.enter_context(tc.tile_pool(name="sorted", bufs=3))
-        grouped_pool = ctx.enter_context(tc.tile_pool(name="grouped", bufs=5))
+        sorted_pool = ctx.enter_context(tc.tile_pool(name="sorted", bufs=4))
+        grouped_pool = ctx.enter_context(tc.tile_pool(name="grouped", bufs=4))
         codes_pool = ctx.enter_context(tc.tile_pool(name="codes", bufs=8))
         rot_pool = ctx.enter_context(tc.tile_pool(name="rot", bufs=3))
         result_pool = ctx.enter_context(tc.tile_pool(name="result", bufs=4))
@@ -310,6 +310,11 @@ def tile_minitransformerlayer_pa_kernel(tc, x, pe, w_qkv, g1, b1, out_0, out_1, 
                 in_=result[:].rearrange("s (h d) -> s h d", d=P),
             )
 
+        def sorted_passes(t):
+            if t < SORT_FROM:
+                return 0
+            return 2 if (t - LEAD - 1) % 3 == 0 else 1
+
         halves = [(n, half) for n in range(len(groups)) for half in range(2)]
         products_order = [(0, 0)]
         for n in range(1, len(groups)):
@@ -328,22 +333,30 @@ def tile_minitransformerlayer_pa_kernel(tc, x, pe, w_qkv, g1, b1, out_0, out_1, 
         quantise_h(0)
         multiply(*products_order[0])
         transpose_weights(*halves[4])
-        normalise(1)
         quantise_weights(*halves[2])
         quantise_weights(*halves[3])
+        multiply(*products_order[1])
         transpose_weights(*halves[5])
-        transpose_h(1)
-        quantise_h(1)
-        quantise_weights(*halves[4])
+        normalise(1)
+        transpose_weights(*halves[6])
         finish(*products_order[0])
-        waiting = [products_order[0]]
-        for t in range(1, len(halves)):
-            for c in range(HALF):
-                multiply(*products_order[t], passes=range(c * HALF, (c + 1) * HALF))
-                if c == 0 and t + LEAD < len(halves):
+        transpose_h(1)
+        quantise_weights(*halves[4])
+        transpose_weights(*halves[7])
+        quantise_h(1)
+        quantise_weights(*halves[5])
+        finish(*products_order[1])
+        quantise_weights(*halves[6])
+        waiting = products_order[:2]
+        for t in range(2, len(halves)):
+            split = 1 if t + LEAD < len(halves) and sorted_passes(t + LEAD) == HALF else HALF
+            for part in range(split):
+                multiply(*products_order[t], passes=range(part * PASSES // split, (part + 1) * PASSES // split))
+                if part < split - 1 and t + LEAD < len(halves):
                     transpose_weights(*halves[t + LEAD], passes=(0,))
-            if SORT_FROM <= t + LEAD + 1 < len(halves):
-                sort_words(*halves[t + LEAD + 1], 0)
+            if t + LEAD + 1 < len(halves):
+                for c in range(sorted_passes(t + LEAD + 1)):
+                    sort_words(*halves[t + LEAD + 1], c)
             if t + LEAD - 1 < len(halves):
                 quantise_weights(*halves[t + LEAD - 1])
             if groups[products_order[t][0]][0] < 2:
@@ -358,6 +371,6 @@ def tile_minitransformerlayer_pa_kernel(tc, x, pe, w_qkv, g1, b1, out_0, out_1, 
             else:
                 add_and_store(*products_order[t], nc.gpsimd)
             if t + LEAD < len(halves):
-                transpose_weights(*halves[t + LEAD], passes=(1,))
+                transpose_weights(*halves[t + LEAD], passes=range(split - 1, HALF))
         for product in waiting:
             add_and_store(*product, nc.vector)

@@ -26,6 +26,7 @@ GROUP_HEADS = GROUP // P
 WORDS = D // 2
 PREFETCH = 4
 SORT_FROM = 8
+HOLD = 10
 LEAD = 6
 HALF = PASSES // 2
 
@@ -45,13 +46,13 @@ def tile_minitransformerlayer_pa_kernel(tc, x, pe, w_qkv, g1, b1, out_0, out_1, 
         grouped_pool = ctx.enter_context(tc.tile_pool(name="grouped", bufs=4))
         codes_pool = ctx.enter_context(tc.tile_pool(name="codes", bufs=8))
         rot_pool = ctx.enter_context(tc.tile_pool(name="rot", bufs=3))
-        result_pool = ctx.enter_context(tc.tile_pool(name="result", bufs=4))
+        result_pool = ctx.enter_context(tc.tile_pool(name="result", bufs=HOLD + 2))
         flip_psum = ctx.enter_context(tc.psum_pool(name="flip_psum", bufs=6))
         acc_psum = ctx.enter_context(tc.psum_pool(name="acc_psum", bufs=2))
         ctx.enter_context(tc.manual_schedule())
 
-        gain_row = const.tile([P, D], BF16)
-        bias_row = const.tile([P, D], BF16)
+        gain_row = sorted_pool.tile([P, D], BF16, tag="in_order", name="gain_row")
+        bias_row = sorted_pool.tile([P, D], BF16, tag="in_order", name="bias_row")
         nc.vector.memset(gain_row[:].bitcast(I32), 0)
         ones = const.tile([P, P], BF16)
         nc.vector.memset(ones[:], 1.0)
@@ -116,7 +117,7 @@ def tile_minitransformerlayer_pa_kernel(tc, x, pe, w_qkv, g1, b1, out_0, out_1, 
         nc.gpsimd.tensor_copy(out=table_b[:, :, :, 1], in_=pe_pairs[:, :, :, 0])
 
         def repeat_on_partitions(row, name):
-            repeated = const.tile([P, D], BF16, name=name)
+            repeated = sorted_pool.tile([P, D], BF16, tag="in_order", name=name)
             for bank in range(D // (2 * BANK)):
                 spread = flip_psum.tile([P, 2 * BANK], BF16, tag="flipped", name="spread")
                 for side in range(2):
@@ -200,7 +201,7 @@ def tile_minitransformerlayer_pa_kernel(tc, x, pe, w_qkv, g1, b1, out_0, out_1, 
         def sort_words(n, half, c):
             words = w_raw[n][:].bitcast(F32).rearrange("p (r w) -> p r w", r=ROWS)
             first = 2 * (half * HALF + c) * P
-            in_order = sorted_pool.tile([P, ROWS, 2, P], F32, name="in_order")
+            in_order = sorted_pool.tile([P, ROWS, 2, P], F32, tag="in_order", name="in_order")
             nc.vector.tensor_copy(
                 out=in_order[:], in_=words[:, :, first : first + 2 * P].rearrange("p r (q u) -> p r u q", u=2)
             )
@@ -267,9 +268,7 @@ def tile_minitransformerlayer_pa_kernel(tc, x, pe, w_qkv, g1, b1, out_0, out_1, 
                     stop=(c == PASSES - 1),
                 )
 
-        rotated = {}
-        waited = const.tile([P, 1], U32)
-        results = {}
+        results = []
 
         def finish(n, b):
             part = groups[n][0]
@@ -295,16 +294,13 @@ def tile_minitransformerlayer_pa_kernel(tc, x, pe, w_qkv, g1, b1, out_0, out_1, 
                     in0=pairs[:, 1].unsqueeze(3).to_broadcast(shape),
                     in1=table_b[:].rearrange("s h (q v) i -> s (h q) v i", v=2),
                 )
-                rotated[(n, b)] = (from_a, from_b)
-            results[(n, b)] = result
+                nc.gpsimd.tensor_add(out=result[:], in0=from_a[:], in1=from_b[:])
+            results.append((n, b, result))
 
-        def add_and_store(n, b, engine):
+        def store():
+            n, b, result = results.pop(0)
             part, head_group = groups[n]
             heads = slice(head_group * GROUP_HEADS, (head_group + 1) * GROUP_HEADS)
-            result = results[(n, b)]
-            if part < 2:
-                from_a, from_b = rotated[(n, b)]
-                engine.tensor_add(out=result[:], in0=from_a[:], in1=from_b[:])
             nc.sync.dma_start(
                 out=outs[part][b, heads].rearrange("h s d -> s h d"),
                 in_=result[:].rearrange("s (h d) -> s h d", d=P),
@@ -347,7 +343,6 @@ def tile_minitransformerlayer_pa_kernel(tc, x, pe, w_qkv, g1, b1, out_0, out_1, 
         quantise_weights(*halves[5])
         finish(*products_order[1])
         quantise_weights(*halves[6])
-        waiting = products_order[:2]
         for t in range(2, len(halves)):
             split = 1 if t + LEAD < len(halves) and sorted_passes(t + LEAD) == HALF else HALF
             for part in range(split):
@@ -359,18 +354,12 @@ def tile_minitransformerlayer_pa_kernel(tc, x, pe, w_qkv, g1, b1, out_0, out_1, 
                     sort_words(*halves[t + LEAD + 1], c)
             if t + LEAD - 1 < len(halves):
                 quantise_weights(*halves[t + LEAD - 1])
-            if groups[products_order[t][0]][0] < 2:
-                if t + LEAD - 1 < len(halves):
-                    nc.gpsimd.tensor_copy(out=waited[:], in_=w_codes[halves[t + LEAD - 1]][:, 0, 0:1])
-                for product in waiting:
-                    add_and_store(*product, nc.gpsimd)
-                waiting = []
             finish(*products_order[t])
-            if groups[products_order[t][0]][0] < 2:
-                waiting.append(products_order[t])
-            else:
-                add_and_store(*products_order[t], nc.gpsimd)
             if t + LEAD < len(halves):
                 transpose_weights(*halves[t + LEAD], passes=range(split - 1, HALF))
-        for product in waiting:
-            add_and_store(*product, nc.vector)
+            loading = (t + LEAD) // 2 + PREFETCH < len(groups)
+            held = HOLD if loading else max(0, len(results) - 2)
+            while len(results) > held:
+                store()
+        while results:
+            store()

@@ -26,7 +26,6 @@ GROUP_HEADS = GROUP // P
 WORDS = D // 2
 PREFETCH = 4
 SORT_FROM = 8
-HOLD = 10
 LEAD = 6
 HALF = PASSES // 2
 
@@ -44,9 +43,9 @@ def tile_minitransformerlayer_pa_kernel(tc, x, pe, w_qkv, g1, b1, out_0, out_1, 
         raw_pool = ctx.enter_context(tc.tile_pool(name="raw", bufs=PREFETCH))
         sorted_pool = ctx.enter_context(tc.tile_pool(name="sorted", bufs=4))
         grouped_pool = ctx.enter_context(tc.tile_pool(name="grouped", bufs=4))
-        codes_pool = ctx.enter_context(tc.tile_pool(name="codes", bufs=8))
+        codes_pool = ctx.enter_context(tc.tile_pool(name="codes", bufs=7))
         rot_pool = ctx.enter_context(tc.tile_pool(name="rot", bufs=3))
-        result_pool = ctx.enter_context(tc.tile_pool(name="result", bufs=HOLD + 2))
+        result_pool = ctx.enter_context(tc.tile_pool(name="result", bufs=15))
         flip_psum = ctx.enter_context(tc.psum_pool(name="flip_psum", bufs=6))
         acc_psum = ctx.enter_context(tc.psum_pool(name="acc_psum", bufs=2))
         ctx.enter_context(tc.manual_schedule())
@@ -108,9 +107,10 @@ def tile_minitransformerlayer_pa_kernel(tc, x, pe, w_qkv, g1, b1, out_0, out_1, 
         pe_pairs = (
             pe_sb[:].rearrange("p (j i) -> p j i", i=2).unsqueeze(1).to_broadcast([P, GROUP_HEADS, P // 2, 2])
         )
-        table_a = const.tile([P, GROUP_HEADS, P], F32)
-        nc.gpsimd.tensor_copy(out=table_a[:], in_=pe_heads)
-        table_b = const.tile([P, GROUP_HEADS, P // 2, 2], F32)
+        tables = const.tile([P, 2, GROUP], F32)
+        table_a = tables[:, 0, :].rearrange("p (h d) -> p h d", d=P)
+        nc.gpsimd.tensor_copy(out=table_a, in_=pe_heads)
+        table_b = tables[:, 1, :].rearrange("p (h j i) -> p h j i", j=P // 2, i=2)
         nc.gpsimd.tensor_scalar(
             out=table_b[:, :, :, 0], in0=pe_pairs[:, :, :, 1], scalar1=-1.0, scalar2=0.0, op0=ALU.mult, op1=ALU.add
         )
@@ -151,18 +151,22 @@ def tile_minitransformerlayer_pa_kernel(tc, x, pe, w_qkv, g1, b1, out_0, out_1, 
             mean_var[b] = mv
             std[b] = root
 
+        centred_x = {}
         h_rows = {}
 
-        def normalise(b):
+        def centre(b):
             centred = const.tile([P, D], F32, name="centred")
             nc.vector.scalar_tensor_tensor(
                 out=centred[:], in0=x_sb[b][:], scalar=mean_var[b][:, 0:1], in1=gain[:], op0=ALU.subtract, op1=ALU.mult
             )
+            centred_x[b] = centred
+
+        def normalise(b):
             rstd = norm.tile([P, 1], F32, name="rstd")
             nc.vector.reciprocal(out=rstd[:], in_=std[b][:])
             h_tile = norm.tile([P, D], BF16, name="h_tile")
             nc.vector.scalar_tensor_tensor(
-                out=h_tile[:], in0=centred[:], scalar=rstd[:], in1=bias[:], op0=ALU.mult, op1=ALU.add
+                out=h_tile[:], in0=centred_x[b][:], scalar=rstd[:], in1=bias[:], op0=ALU.mult, op1=ALU.add
             )
             h_rows[b] = h_tile
 
@@ -281,20 +285,13 @@ def tile_minitransformerlayer_pa_kernel(tc, x, pe, w_qkv, g1, b1, out_0, out_1, 
                 )
             else:
                 pairs = acc[:].rearrange("s (v i p) -> s i p v", v=2, i=2)
-                shape = [P, P, 2, 2]
-                from_a = rot_pool.tile([P, GROUP], F32, name="from_a")
+                from_ab = rot_pool.tile([P, 2, GROUP], F32, name="from_ab")
                 nc.vector.tensor_mul(
-                    out=from_a[:].rearrange("s (p v i) -> s p v i", v=2, i=2),
-                    in0=pairs[:, 0].unsqueeze(3).to_broadcast(shape),
-                    in1=table_a[:].rearrange("s h (q v i) -> s (h q) v i", v=2, i=2),
+                    out=from_ab[:].rearrange("s k (p v i) -> s k p v i", v=2, i=2),
+                    in0=pairs.unsqueeze(4).to_broadcast([P, 2, P, 2, 2]),
+                    in1=tables[:].rearrange("s k (q v i) -> s k q v i", v=2, i=2),
                 )
-                from_b = rot_pool.tile([P, GROUP], F32, name="from_b")
-                nc.vector.tensor_mul(
-                    out=from_b[:].rearrange("s (p v i) -> s p v i", v=2, i=2),
-                    in0=pairs[:, 1].unsqueeze(3).to_broadcast(shape),
-                    in1=table_b[:].rearrange("s h (q v) i -> s (h q) v i", v=2),
-                )
-                nc.gpsimd.tensor_add(out=result[:], in0=from_a[:], in1=from_b[:])
+                nc.gpsimd.tensor_add(out=result[:], in0=from_ab[:, 0, :], in1=from_ab[:, 1, :])
             results.append((n, b, result))
 
         def store():
@@ -319,6 +316,7 @@ def tile_minitransformerlayer_pa_kernel(tc, x, pe, w_qkv, g1, b1, out_0, out_1, 
         token_statistics(0)
         transpose_weights(*halves[0])
         transpose_weights(*halves[1])
+        centre(0)
         normalise(0)
         transpose_h(0)
         transpose_weights(*halves[2])
@@ -330,18 +328,19 @@ def tile_minitransformerlayer_pa_kernel(tc, x, pe, w_qkv, g1, b1, out_0, out_1, 
         multiply(*products_order[0])
         transpose_weights(*halves[4])
         quantise_weights(*halves[2])
+        centre(1)
         quantise_weights(*halves[3])
         multiply(*products_order[1])
-        transpose_weights(*halves[5])
         normalise(1)
-        transpose_weights(*halves[6])
-        finish(*products_order[0])
+        transpose_weights(*halves[5])
         transpose_h(1)
+        finish(*products_order[0])
         quantise_weights(*halves[4])
-        transpose_weights(*halves[7])
+        transpose_weights(*halves[6])
         quantise_h(1)
-        quantise_weights(*halves[5])
         finish(*products_order[1])
+        quantise_weights(*halves[5])
+        transpose_weights(*halves[7])
         quantise_weights(*halves[6])
         for t in range(2, len(halves)):
             split = 1 if t + LEAD < len(halves) and sorted_passes(t + LEAD) == HALF else HALF
@@ -358,8 +357,5 @@ def tile_minitransformerlayer_pa_kernel(tc, x, pe, w_qkv, g1, b1, out_0, out_1, 
             if t + LEAD < len(halves):
                 transpose_weights(*halves[t + LEAD], passes=range(split - 1, HALF))
             loading = (t + LEAD) // 2 + PREFETCH < len(groups)
-            held = HOLD if loading else max(0, len(results) - 2)
-            while len(results) > held:
+            while results and not loading:
                 store()
-        while results:
-            store()

@@ -46,8 +46,8 @@ def tile_minitransformerlayer_pa_kernel(tc, x, pe, w_qkv, g1, b1, out_0, out_1, 
         codes_pool = ctx.enter_context(tc.tile_pool(name="codes", bufs=7))
         rot_pool = ctx.enter_context(tc.tile_pool(name="rot", bufs=3))
         result_pool = ctx.enter_context(tc.tile_pool(name="result", bufs=15))
-        flip_psum = ctx.enter_context(tc.psum_pool(name="flip_psum", bufs=6))
-        acc_psum = ctx.enter_context(tc.psum_pool(name="acc_psum", bufs=2))
+        flip_psum = ctx.enter_context(tc.psum_pool(name="flip_psum", bufs=5))
+        acc_psum = ctx.enter_context(tc.psum_pool(name="acc_psum", bufs=3))
         ctx.enter_context(tc.manual_schedule())
 
         gain_row = sorted_pool.tile([P, D], BF16, tag="in_order", name="gain_row")
@@ -330,9 +330,11 @@ def tile_minitransformerlayer_pa_kernel(tc, x, pe, w_qkv, g1, b1, out_0, out_1, 
         quantise_weights(*halves[2])
         centre(1)
         quantise_weights(*halves[3])
-        multiply(*products_order[1])
+        multiply(*products_order[1], passes=range(0, 2))
+        transpose_weights(*halves[5], passes=(0,))
+        multiply(*products_order[1], passes=range(2, 4))
         normalise(1)
-        transpose_weights(*halves[5])
+        transpose_weights(*halves[5], passes=(1,))
         transpose_h(1)
         finish(*products_order[0])
         quantise_weights(*halves[4])

from contextlib import ExitStack

import concourse.mybir as mybir
from concourse.masks import make_identity

F32 = mybir.dt.float32
BF16 = mybir.dt.bfloat16
I32 = mybir.dt.int32
U32 = mybir.dt.uint32
U8 = mybir.dt.uint8
FP8X4 = mybir.dt.float8_e4m3fn_x4
ALU = mybir.AluOpType

P = 128
BATCH = 2
D = 2048
HEADS = 16
E = HEADS * P
EPS = 1e-5
PACK = 4
PASSES = D // (P * PACK)
BANK = 512
GROUP = BANK
ROWS = GROUP // P
GROUP_HEADS = GROUP // P
WORDS = D // 2
PREFETCH = 4
SORT_FROM = 8
LEAD = 6
HALF = PASSES // 2

FLOPS = 2 * BATCH * P * D * 3 * E


def tile_minitransformerlayer_pa_kernel(tc, x, pe, w_qkv, g1, b1, out_0, out_1, out_2):
    nc = tc.nc
    outs = (out_0, out_1, out_2)
    groups = [(part, head_group) for head_group in range(HEADS // GROUP_HEADS) for part in range(3)]

    with ExitStack() as ctx:
        const = ctx.enter_context(tc.tile_pool(name="const", bufs=1))
        norm = ctx.enter_context(tc.tile_pool(name="norm", bufs=BATCH))
        raw_pool = ctx.enter_context(tc.tile_pool(name="raw", bufs=PREFETCH))
        sorted_pool = ctx.enter_context(tc.tile_pool(name="sorted", bufs=4))
        grouped_pool = ctx.enter_context(tc.tile_pool(name="grouped", bufs=4))
        codes_pool = ctx.enter_context(tc.tile_pool(name="codes", bufs=7))
        rot_pool = ctx.enter_context(tc.tile_pool(name="rot", bufs=3))
        result_pool = ctx.enter_context(tc.tile_pool(name="result", bufs=15))
        flip_psum = ctx.enter_context(tc.psum_pool(name="flip_psum", bufs=5))
        acc_psum = ctx.enter_context(tc.psum_pool(name="acc_psum", bufs=3))
        ctx.enter_context(tc.manual_schedule())

        gain_row = sorted_pool.tile([P, D], BF16, tag="in_order", name="gain_row")
        bias_row = sorted_pool.tile([P, D], BF16, tag="in_order", name="bias_row")
        nc.vector.memset(gain_row[:].bitcast(I32), 0)
        ones = const.tile([P, P], BF16)
        nc.vector.memset(ones[:], 1.0)
        nc.vector.memset(bias_row[:].bitcast(I32), 0)
        one = const.tile([P, 1], F32)
        nc.vector.memset(one[:], 1.0)
        warm = const.tile([P, 1], F32)
        nc.scalar.sqrt(out=warm[:], in_=one[:])
        pe_sb = const.tile([P, P], BF16)
        ident_f32 = const.tile([P, P], F32)
        make_identity(nc, ident_f32[:])

        x_sb = {}

        def load_tokens(b, c):
            cols = slice(c * BANK, (c + 1) * BANK)
            nc.sync.dma_start(out=x_sb[b][:, cols], in_=x[b][:, cols])

        for b in range(BATCH):
            x_tile = norm.tile([P, D], BF16, name="x_tile")
            x_sb[b] = x_tile

        w_raw = {}

        def load_weights(n, pieces=1):
            part, head_group = groups[n]
            first = part * E + head_group * GROUP
            raw = raw_pool.tile([P, ROWS * D], BF16, name="raw")
            rows = w_qkv[first : first + GROUP, :].rearrange("(p r) k -> p r k", r=ROWS)
            width = D // pieces
            for piece in range(pieces):
                cols = slice(piece * width, (piece + 1) * width)
                nc.sync.dma_start(
                    out=raw[:].rearrange("p (r k) -> p r k", r=ROWS)[:, :, cols], in_=rows[:, :, cols]
                )
            w_raw[n] = raw

        load_tokens(0, 0)
        load_tokens(0, 1)
        nc.sync.dma_start(out=gain_row[0:1, :], in_=g1.rearrange("(o d) -> o d", o=1))
        nc.sync.dma_start(out=bias_row[0:1, :], in_=b1.rearrange("(o d) -> o d", o=1))
        load_tokens(0, 2)
        load_tokens(0, 3)
        load_weights(0, 2)
        for c in range(D // BANK):
            load_tokens(1, c)
        nc.sync.dma_start(out=pe_sb[:], in_=pe)
        load_weights(1, 2)
        for n in range(2, PREFETCH):
            load_weights(n)

        pe_heads = pe_sb[:].unsqueeze(1).to_broadcast([P, GROUP_HEADS, P])
        pe_pairs = (
            pe_sb[:].rearrange("p (j i) -> p j i", i=2).unsqueeze(1).to_broadcast([P, GROUP_HEADS, P // 2, 2])
        )
        tables = const.tile([P, 2, GROUP], F32)
        table_a = tables[:, 0, :].rearrange("p (h d) -> p h d", d=P)
        nc.gpsimd.tensor_copy(out=table_a, in_=pe_heads)
        table_b = tables[:, 1, :].rearrange("p (h j i) -> p h j i", j=P // 2, i=2)
        nc.gpsimd.tensor_scalar(
            out=table_b[:, :, :, 0], in0=pe_pairs[:, :, :, 1], scalar1=-1.0, scalar2=0.0, op0=ALU.mult, op1=ALU.add
        )
        nc.gpsimd.tensor_copy(out=table_b[:, :, :, 1], in_=pe_pairs[:, :, :, 0])

        def repeat_on_partitions(row, name):
            repeated = sorted_pool.tile([P, D], BF16, tag="in_order", name=name)
            for bank in range(D // (2 * BANK)):
                spread = flip_psum.tile([P, 2 * BANK], BF16, tag="flipped", name="spread")
                for side in range(2):
                    first = (2 * bank + side) * BANK
                    nc.tensor.matmul(
                        out=spread[:, side * BANK : (side + 1) * BANK],
                        lhsT=ones[:],
                        rhs=row[:, first : first + BANK],
                        start=True,
                        stop=True,
                    )
                nc.scalar.copy(out=repeated[:, 2 * bank * BANK : 2 * (bank + 1) * BANK], in_=spread[:])
            return repeated

        gain = repeat_on_partitions(gain_row, "gain")
        bias = repeat_on_partitions(bias_row, "bias")

        mean_var = {}
        std = {}

        def token_statistics(b):
            stats = norm.tile([P, D // BANK, 6], F32, name="stats")
            for c in range(D // BANK):
                nc.vector.bn_stats(out=stats[:, c, :], in_=x_sb[b][:, c * BANK : (c + 1) * BANK])
            mv = norm.tile([P, 2], F32, name="mv")
            nc.vector.bn_aggr(out=mv[:], in_=stats[:].rearrange("p c s -> p (c s)"))
            var_eps = norm.tile([P, 1], F32, name="var_eps")
            nc.vector.tensor_scalar_add(out=var_eps[:], in0=mv[:, 1:2], scalar1=EPS)
            root = norm.tile([P, 1], F32, name="root")
            nc.scalar.sqrt(out=root[:], in_=var_eps[:])
            mean_var[b] = mv
            std[b] = root

        centred_x = {}
        h_rows = {}

        def centre(b):
            centred = const.tile([P, D], F32, name="centred")
            nc.vector.scalar_tensor_tensor(
                out=centred[:], in0=x_sb[b][:], scalar=mean_var[b][:, 0:1], in1=gain[:], op0=ALU.subtract, op1=ALU.mult
            )
            centred_x[b] = centred

        def normalise(b):
            rstd = norm.tile([P, 1], F32, name="rstd")
            nc.vector.reciprocal(out=rstd[:], in_=std[b][:])
            h_tile = norm.tile([P, D], BF16, name="h_tile")
            nc.vector.scalar_tensor_tensor(
                out=h_tile[:], in0=centred_x[b][:], scalar=rstd[:], in1=bias[:], op0=ALU.mult, op1=ALU.add
            )
            h_rows[b] = h_tile

        h_grouped = const.tile([P, BATCH, PASSES, P, PACK], BF16, align_bytes=64)
        h_codes = const.tile([P, BATCH, PASSES * P], U32, align_bytes=64)
        h_scales = const.tile([P, BATCH, PASSES * P], U8, align_bytes=64)

        def transpose_h(b):
            words = h_rows[b][:].bitcast(F32)
            for pair in range(HALF):
                flipped_h = flip_psum.tile([P, HALF, 2, P], F32, tag="flipped", name="flipped_h")
                for c in range(HALF):
                    first = (pair * HALF + c) * 2 * P
                    for u in range(2):
                        nc.tensor.transpose(
                            flipped_h[:, c, u, :], words[:, first + u : first + 2 * P : 2], ident_f32[:]
                        )
                nc.scalar.copy(
                    out=h_grouped[:, b, pair * HALF : (pair + 1) * HALF, :, :]
                    .rearrange("p c r t -> p (c r t)")
                    .bitcast(F32)
                    .rearrange("p (c r u) -> p c r u", c=HALF, u=2),
                    in_=flipped_h[:].rearrange("p c u r -> p c r u"),
                )

        def quantise_h(b):
            nc.vector.quantize_mx(
                out=h_codes[:, b, :].bitcast(FP8X4),
                scales=h_scales[:, b, :],
                in_=h_grouped[:, b].rearrange("p c r t -> p (c r t)"),
            )

        w_grouped = {}
        w_sorted = {}

        def sort_words(n, half, c):
            words = w_raw[n][:].bitcast(F32).rearrange("p (r w) -> p r w", r=ROWS)
            first = 2 * (half * HALF + c) * P
            in_order = sorted_pool.tile([P, ROWS, 2, P], F32, tag="in_order", name="in_order")
            nc.vector.tensor_copy(
                out=in_order[:], in_=words[:, :, first : first + 2 * P].rearrange("p r (q u) -> p r u q", u=2)
            )
            w_sorted[(n, half, c)] = in_order

        def transpose_weights(n, half, passes=range(HALF)):
            words = w_raw[n][:].bitcast(F32)
            if 0 in passes:
                grouped = grouped_pool.tile([P, HALF, GROUP * PACK], BF16, align_bytes=64, name="grouped")
                w_grouped[(n, half)] = grouped
            grouped = w_grouped[(n, half)]
            for c in passes:
                grouped_words = grouped[:, c, :].bitcast(F32)
                for side in range(2):
                    flipped = flip_psum.tile([P, 2, BANK // 2], F32, tag="flipped", name="flipped")
                    for u in range(2):
                        for r in range(2):
                            first = (2 * side + r) * WORDS + 2 * (half * HALF + c) * P
                            if (n, half, c) in w_sorted:
                                column_words = w_sorted[(n, half, c)][:, 2 * side + r, u, :]
                            else:
                                column_words = words[:, first + u : first + 2 * P : 2]
                            nc.tensor.transpose(flipped[:, u, r * P : (r + 1) * P], column_words, ident_f32[:])
                    nc.scalar.copy(
                        out=grouped_words[:, side * BANK : (side + 1) * BANK].rearrange("p (n u) -> p n u", u=2),
                        in_=flipped[:].rearrange("p u n -> p n u"),
                    )
            if half == 1 and HALF - 1 in passes and n + PREFETCH < len(groups):
                load_weights(n + PREFETCH)

        w_codes = {}
        w_scales = {}

        def quantise_weights(n, half):
            codes = codes_pool.tile([P, HALF, GROUP], U32, align_bytes=64, name="codes")
            scales = codes_pool.tile([P, HALF, GROUP], U8, align_bytes=64, name="scales")
            nc.vector.quantize_mx(
                out=codes[:].rearrange("p c n -> p (c n)").bitcast(FP8X4),
                scales=scales[:].rearrange("p c n -> p (c n)"),
                in_=w_grouped[(n, half)][:].rearrange("p c n -> p (c n)"),
            )
            w_codes[(n, half)] = codes
            w_scales[(n, half)] = scales

        products = {}

        def multiply(n, b, passes=range(PASSES)):
            if 0 in passes:
                if n >= len(groups) - 1:
                    acc = flip_psum.tile([P, BANK], F32, tag="flipped", name="acc")
                else:
                    acc = acc_psum.tile([P, BANK], F32, name="acc")
                products[(n, b)] = acc
            acc = products[(n, b)]
            for c in passes:
                tokens = slice(c * P, (c + 1) * P)
                nc.tensor.matmul_mx(
                    out=acc[:],
                    lhsT=h_codes[:, b, tokens].bitcast(FP8X4),
                    lhsT_scale=h_scales[:, b, tokens],
                    rhs=w_codes[(n, c // HALF)][:, c % HALF, :].bitcast(FP8X4),
                    rhs_scale=w_scales[(n, c // HALF)][:, c % HALF, :],
                    start=(c == 0),
                    stop=(c == PASSES - 1),
                )

        results = []

        def finish(n, b):
            part = groups[n][0]
            acc = products[(n, b)]
            result = result_pool.tile([P, GROUP], F32, name="result")
            if part == 2:
                nc.scalar.copy(
                    out=result[:].rearrange("s (p r) -> s p r", r=ROWS),
                    in_=acc[:].rearrange("s (r p) -> s p r", r=ROWS),
                )
            else:
                pairs = acc[:].rearrange("s (v i p) -> s i p v", v=2, i=2)
                from_ab = rot_pool.tile([P, 2, GROUP], F32, name="from_ab")
                nc.vector.tensor_mul(
                    out=from_ab[:].rearrange("s k (p v i) -> s k p v i", v=2, i=2),
                    in0=pairs.unsqueeze(4).to_broadcast([P, 2, P, 2, 2]),
                    in1=tables[:].rearrange("s k (q v i) -> s k q v i", v=2, i=2),
                )
                nc.gpsimd.tensor_add(out=result[:], in0=from_ab[:, 0, :], in1=from_ab[:, 1, :])
            results.append((n, b, result))

        def store():
            n, b, result = results.pop(0)
            part, head_group = groups[n]
            heads = slice(head_group * GROUP_HEADS, (head_group + 1) * GROUP_HEADS)
            nc.sync.dma_start(
                out=outs[part][b, heads].rearrange("h s d -> s h d"),
                in_=result[:].rearrange("s (h d) -> s h d", d=P),
            )

        def sorted_passes(t):
            if t < SORT_FROM:
                return 0
            return 2 if (t - LEAD - 1) % 3 == 0 else 1

        halves = [(n, half) for n in range(len(groups)) for half in range(2)]
        products_order = [(0, 0)]
        for n in range(1, len(groups)):
            products_order += [(n, 0), (n - 1, 1)]
        products_order.append((len(groups) - 1, 1))
        token_statistics(0)
        transpose_weights(*halves[0])
        transpose_weights(*halves[1])
        centre(0)
        normalise(0)
        transpose_h(0)
        transpose_weights(*halves[2])
        transpose_weights(*halves[3])
        token_statistics(1)
        quantise_weights(*halves[0])
        quantise_weights(*halves[1])
        quantise_h(0)
        multiply(*products_order[0])
        transpose_weights(*halves[4])
        quantise_weights(*halves[2])
        centre(1)
        quantise_weights(*halves[3])
        multiply(*products_order[1], passes=range(0, 2))
        transpose_weights(*halves[5], passes=(0,))
        multiply(*products_order[1], passes=range(2, 4))
        normalise(1)
        transpose_weights(*halves[5], passes=(1,))
        transpose_h(1)
        finish(*products_order[0])
        quantise_weights(*halves[4])
        transpose_weights(*halves[6])
        quantise_h(1)
        finish(*products_order[1])
        quantise_weights(*halves[5])
        transpose_weights(*halves[7])
        quantise_weights(*halves[6])
        for t in range(2, len(halves)):
            split = 1 if t + LEAD < len(halves) and sorted_passes(t + LEAD) == HALF else HALF
            for part in range(split):
                multiply(*products_order[t], passes=range(part * PASSES // split, (part + 1) * PASSES // split))
                if part < split - 1 and t + LEAD < len(halves):
                    transpose_weights(*halves[t + LEAD], passes=(0,))
            if t + LEAD + 1 < len(halves):
                for c in range(sorted_passes(t + LEAD + 1)):
                    sort_words(*halves[t + LEAD + 1], c)
            if t + LEAD - 1 < len(halves):
                quantise_weights(*halves[t + LEAD - 1])
            finish(*products_order[t])
            if t + LEAD < len(halves):
                transpose_weights(*halves[t + LEAD], passes=range(split - 1, HALF))
            loading = (t + LEAD) // 2 + PREFETCH < len(groups)
            while results and not loading:
                store()
